import numpy as np
import ml_dtypes


def mxq(x, axis, fmt="e4m3"):
    dtype, down = {"e4m3": (ml_dtypes.float8_e4m3fn, 7), "e5m2": (ml_dtypes.float8_e5m2, 14)}[fmt]
    v = np.moveaxis(np.asarray(x, np.float32).astype(ml_dtypes.bfloat16).astype(np.float64), axis, -1)
    blocks = v.reshape(v.shape[:-1] + (-1, 32))
    amax = np.abs(blocks).max(-1, keepdims=True)
    byte = np.maximum(np.where(amax > 0, np.frexp(amax)[1] - 1 + 127, 0) - down, 1)
    scale = np.exp2(byte - 127.0)
    codes = (blocks / scale).astype(np.float32).astype(dtype).astype(np.float64)
    return np.moveaxis((codes * scale).reshape(v.shape), -1, axis)


WIDE = False


def mx_kscale(k):
    if not WIDE:
        return np.ones(k)
    levels = np.array([10, -10, 5, -5, 0])
    a = np.random.permutation(np.resize(levels, k // 512 * 4)).reshape(k // 512, 4)
    idx = np.arange(k)
    return np.exp2(a[idx // 512, idx % 128 // 32])


BF16 = ml_dtypes.bfloat16


def bf(x):
    return np.asarray(x, np.float32).astype(BF16)


def f64(x):
    return np.asarray(x).astype(np.float64)


E2M1 = np.array([0.0, 0.5, 1.0, 1.5, 2.0, 3.0, 4.0, 6.0, -0.0, -0.5, -1.0, -1.5, -2.0, -3.0, -4.0, -6.0])


def pack_weight(w, fmt):
    k, n = w.shape
    w = f64(bf(w)).reshape(k // 32, 32, n)
    amax = np.abs(w).max(1)
    if fmt == "e4m3":
        byte = np.frexp(amax)[1] - 1 + 127 - 7
    else:
        mant, ex = np.frexp(amax / 6.0)
        byte = np.where(mant > 0.5, ex, ex - 1) + 127
    byte = np.clip(np.where(amax > 0, byte, 1), 1, 254)
    scaled = (w * np.exp2(127.0 - byte)[:, None, :]).reshape(k, n).astype(np.float32)
    by_word = np.ascontiguousarray(scaled.reshape(k // 512, 128, 4, n).transpose(0, 1, 3, 2))
    if fmt == "e4m3":
        words = by_word.astype(ml_dtypes.float8_e4m3fn).view(np.uint8)
    else:
        c = by_word.astype(ml_dtypes.float4_e2m1fn).view(np.uint8) & 0xF
        words = c[..., 0::2] | (c[..., 1::2] << 4)
    return np.ascontiguousarray(words), np.ascontiguousarray(byte.astype(np.uint8).reshape(k // 512, 16, n))


def unpack_weight(words, scales, fmt):
    g, p, n, _ = words.shape
    if fmt == "e4m3":
        vals = np.ascontiguousarray(words).view(ml_dtypes.float8_e4m3fn).astype(np.float64)
    else:
        nib = np.empty((g, p, n, 4), np.uint8)
        nib[..., 0::2] = words & 0xF
        nib[..., 1::2] = words >> 4
        vals = E2M1[nib]
    vals = vals * np.repeat(np.exp2(scales.astype(np.float64) - 127.0), 8, axis=1)[..., None]
    return vals.transpose(0, 1, 3, 2).reshape(g * 512, n)


B, C, CI, N = 1, 768, 8192, 512
EPS = 1e-5


def setup_inputs():
    s, t = mx_kscale(N), mx_kscale(CI)
    r = np.random.standard_normal
    affinity = bf(r((B, N, N)) * 0.2 * s[None, None, :])
    g_x = bf(r((B, N, CI)) / s[None, :, None] * t[None, None, :])
    w = r((C, CI)) * 1.5 / (0.2 * np.sqrt(N) * np.sqrt(CI)) / t[None, :]
    w_w_words, w_w_scales = pack_weight(np.ascontiguousarray(w.T), "e4m3")
    return {"affinity": affinity,
            "g_x": g_x,
            "w_w_words": w_w_words,
            "w_w_scales": w_w_scales,
            "w_b": bf(r(C) * 0.3),
            "bn_gamma": bf(r(C)),
            "bn_beta": bf(r(C) * 0.5),
            "bn_mean": bf(r(C) * 0.5),
            "bn_var": bf(np.random.uniform(0.5, 1.5, C)),
            "x": bf(r((B, C, N)))}


def reference(affinity, g_x, w_w_words, w_w_scales, w_b, bn_gamma, bn_beta, bn_mean, bn_var, x):
    y = (mxq(f64(affinity), 2, "e4m3") @ mxq(f64(g_x), 1, "e4m3")).transpose(0, 2, 1)
    wy = (unpack_weight(w_w_words, w_w_scales, "e4m3").T @ mxq(y, 1, "e4m3")) + f64(w_b)[None, :, None]
    inv_std = 1.0 / np.sqrt(f64(bn_var) + EPS)
    wy = f64(bn_gamma)[None, :, None] * (wy - f64(bn_mean)[None, :, None]) * inv_std[None, :, None] + f64(bn_beta)[None, :, None]
    return wy + f64(x)

@@ -1,0 +1,258 @@
+from contextlib import ExitStack
+
+import concourse.mybir as mybir
+from concourse.masks import make_identity
+
+F32 = mybir.dt.float32
+BF16 = mybir.dt.bfloat16
+I32 = mybir.dt.int32
+U32 = mybir.dt.uint32
+U8 = mybir.dt.uint8
+FP8X4 = mybir.dt.float8_e4m3fn_x4
+ALU = mybir.AluOpType
+ACT = mybir.ActivationFunctionType
+
+P = 128
+PACK = 4
+K_PASS = P * PACK
+POINTS = 512
+INNER = 8192
+CHANNELS = 768
+EPS = 1e-5
+
+ROUNDS = INNER // K_PASS
+POINT_BLOCKS = POINTS // P
+C_TILES = CHANNELS // P
+CHUNK_ROUNDS = 2
+CHUNKS = ROUNDS // CHUNK_ROUNDS
+PLANES = 4
+QUADRANTS = 4
+VECTORS = 5
+
+FLOPS = 2 * POINTS * POINTS * INNER + 2 * CHANNELS * INNER * POINTS
+
+
+def tile_sgcam_pb_k_kernel(
+    tc, affinity, g_x, w_w_words, w_w_scales, w_b, bn_gamma, bn_beta, bn_mean, bn_var, x, out
+):
+    nc = tc.nc
+    with ExitStack() as ctx:
+        keep = ctx.enter_context(tc.tile_pool(name="keep", bufs=1))
+        g_pool = ctx.enter_context(tc.tile_pool(name="g_pool", bufs=CHUNKS))
+        w_pool = ctx.enter_context(tc.tile_pool(name="w_pool", bufs=CHUNKS))
+        grouped_pool = ctx.enter_context(tc.tile_pool(name="grouped_pool", bufs=2))
+        codes_pool = ctx.enter_context(tc.tile_pool(name="codes_pool", bufs=3))
+        acc_pool = ctx.enter_context(tc.psum_pool(name="acc_pool", bufs=1))
+        bank_pool = ctx.enter_context(tc.psum_pool(name="bank_pool", bufs=2))
+        ctx.enter_context(tc.manual_schedule())
+
+        w_planes = keep.tile([P, ROUNDS // PLANES, CHANNELS], U8, align_bytes=64)
+        nc.vector.memset(w_planes[:].rearrange("p s n -> p (s n)").bitcast(I32), 0)
+        vec_rows = keep.tile([P, P], BF16)
+        nc.vector.memset(vec_rows[:], 0.0)
+        eps_col = keep.tile([P, 1], F32)
+        nc.vector.memset(eps_col[:], EPS)
+        ident_f32 = keep.tile([P, P], F32)
+        make_identity(nc, ident_f32[:])
+        ident_bf16 = keep.tile([P, P], BF16)
+        make_identity(nc, ident_bf16[:])
+
+        a_rows = keep.tile([P, POINT_BLOCKS, POINTS], BF16)
+        nc.sync.dma_start(out=a_rows[:], in_=affinity[0].rearrange("(b p) m -> p b m", p=P))
+
+        g_raw = []
+        w_words = []
+
+        def load_g(k):
+            width = CHUNK_ROUNDS * K_PASS
+            raw = g_pool.tile([P, PACK, width], BF16, name="g_raw")
+            nc.sync.dma_start(
+                out=raw[:],
+                in_=g_x[0][:, k * width : (k + 1) * width].rearrange("(p j) c -> p j c", j=PACK),
+            )
+            g_raw.append(raw)
+
+        def load_w_planes(s):
+            for quad in range(QUADRANTS):
+                nc.sync.dma_start(
+                    out=w_planes[32 * quad : 32 * quad + PLANES * 4, s, :].bitcast(I32),
+                    in_=w_w_scales[PLANES * s : PLANES * (s + 1), 4 * quad : 4 * quad + 4, :].bitcast(I32),
+                )
+
+        def load_w(k):
+            words = w_pool.tile([P, CHUNK_ROUNDS, CHANNELS], U32, name="w_words", align_bytes=64)
+            nc.sync.dma_start(
+                out=words[:].bitcast(I32),
+                in_=w_w_words[CHUNK_ROUNDS * k : CHUNK_ROUNDS * (k + 1)]
+                .rearrange("g p n t -> p g (n t)")
+                .bitcast(I32),
+            )
+            w_words.append(words)
+
+        load_g(0)
+        load_g(1)
+        for k in range(CHUNKS):
+            if (k * CHUNK_ROUNDS) % PLANES == 0:
+                load_w_planes(k * CHUNK_ROUNDS // PLANES)
+            load_w(k)
+            if k + 2 < CHUNKS:
+                load_g(k + 2)
+        x_rows = keep.tile([P, C_TILES, POINTS], BF16)
+        nc.sync.dma_start(out=x_rows[:], in_=x[0].rearrange("(c p) n -> p c n", p=P))
+
+        for v, vec in enumerate((w_b, bn_gamma, bn_beta, bn_mean, bn_var)):
+            nc.scalar.dma_start(
+                out=vec_rows[C_TILES * v : C_TILES * (v + 1), :], in_=vec.rearrange("(c p) -> c p", p=P)
+            )
+        warm = keep.tile([P, 1], F32)
+        nc.scalar.sqrt(out=warm[:], in_=eps_col[:])
+
+        a_grouped = keep.tile([P, POINTS, PACK], BF16, align_bytes=64)
+        a_grouped_words = a_grouped[:].rearrange("p n t -> p (n t)").bitcast(F32).rearrange("p (n u) -> p n u", u=2)
+        half_points = POINTS // 2
+        for h in range(2):
+            a_bank = bank_pool.tile([P, 2, half_points], F32, name="a_bank", tag="bank")
+            for u in range(2):
+                for i in range(half_points // P):
+                    b = h * (half_points // P) + i
+                    nc.tensor.transpose(
+                        a_bank[:, u, i * P : (i + 1) * P],
+                        a_rows[:, b, :].bitcast(F32)[:, u : POINTS // 2 : 2],
+                        ident_f32[:],
+                    )
+            nc.scalar.copy(
+                out=a_grouped_words[:, h * half_points : (h + 1) * half_points, :],
+                in_=a_bank[:].rearrange("p u n -> p n u"),
+            )
+        a_codes = keep.tile([P, POINTS], U32, align_bytes=64)
+        a_scales = keep.tile([P, POINTS], U8, align_bytes=64)
+
+        vec_bank = bank_pool.tile([P, P], BF16, name="vec_bank", tag="bank")
+        nc.tensor.transpose(vec_bank[:], vec_rows[:], ident_bf16[:])
+        vec_cols = keep.tile([P, VECTORS, C_TILES], F32)
+        nc.scalar.copy(out=vec_cols[:].rearrange("p v c -> p (v c)"), in_=vec_bank[:, 0 : VECTORS * C_TILES])
+        std = keep.tile([P, C_TILES], F32)
+        nc.scalar.activation(out=std[:], in_=vec_cols[:, 4, :], func=ACT.Sqrt, bias=eps_col[:, 0:1], scale=1.0)
+        bn_scale = keep.tile([P, C_TILES], F32)
+        bn_shift = keep.tile([P, C_TILES], F32)
+
+        def fold_batch_norm():
+            nc.vector.reciprocal(out=bn_scale[:], in_=std[:])
+            nc.vector.tensor_sub(out=bn_shift[:], in0=vec_cols[:, 0, :], in1=vec_cols[:, 3, :])
+            nc.vector.tensor_mul(out=bn_scale[:], in0=bn_scale[:], in1=vec_cols[:, 1, :])
+            nc.vector.tensor_mul(out=bn_shift[:], in0=bn_shift[:], in1=bn_scale[:])
+            nc.vector.tensor_add(out=bn_shift[:], in0=bn_shift[:], in1=vec_cols[:, 2, :])
+
+        x_shifted = keep.tile([P, C_TILES, POINTS], F32)
+
+        def shift_x():
+            for c in range(C_TILES):
+                nc.scalar.activation(
+                    out=x_shifted[:, c, :], in_=x_rows[:, c, :], func=ACT.Identity,
+                    bias=bn_shift[:, c : c + 1], scale=1.0,
+                )
+
+        g_grouped = {}
+        g_codes = {}
+        g_scales = {}
+        y_grouped = {}
+        y_codes = {}
+        y_scales = {}
+        acc = []
+        for c in range(C_TILES):
+            acc_c = acc_pool.tile([P, POINTS], F32, name="acc%d" % c)
+            acc.append(acc_c)
+
+        def regroup_g(g):
+            raw = g_raw[g // CHUNK_ROUNDS]
+            first = (g % CHUNK_ROUNDS) * K_PASS
+            grouped = grouped_pool.tile([P, PACK, P, PACK], BF16, name="g_grouped", align_bytes=64)
+            nc.vector.tensor_copy(
+                out=grouped[:].rearrange("p t q j -> p q j t"),
+                in_=raw[:, :, first : first + K_PASS].rearrange("p j (q t) -> p q j t", t=PACK),
+            )
+            g_grouped[g] = grouped
+
+        def quantise_g(g):
+            codes = codes_pool.tile([P, K_PASS], U32, name="g_codes", align_bytes=64)
+            scales = codes_pool.tile([P, K_PASS], U8, name="g_scales", align_bytes=64)
+            nc.vector.quantize_mx(
+                out=codes[:].bitcast(FP8X4),
+                scales=scales[:],
+                in_=g_grouped[g][:].rearrange("p t q j -> p (t q j)"),
+            )
+            g_codes[g] = codes
+            g_scales[g] = scales
+
+        def first_product(g, blocks):
+            if g not in y_grouped:
+                grouped = grouped_pool.tile([P, POINTS, PACK], BF16, name="y_grouped", align_bytes=64)
+                y_grouped[g] = grouped
+            for b in blocks:
+                y_bank = bank_pool.tile([P, PACK, P], F32, name="y_bank", tag="bank")
+                for t in range(PACK):
+                    nc.tensor.matmul_mx(
+                        out=y_bank[:, t, :],
+                        lhsT=g_codes[g][:, t * P : (t + 1) * P].bitcast(FP8X4),
+                        lhsT_scale=g_scales[g][:, t * P : (t + 1) * P],
+                        rhs=a_codes[:, b * P : (b + 1) * P].bitcast(FP8X4),
+                        rhs_scale=a_scales[:, b * P : (b + 1) * P],
+                        start=True,
+                        stop=True,
+                    )
+                nc.scalar.copy(
+                    out=y_grouped[g][:, b * P : (b + 1) * P, :], in_=y_bank[:].rearrange("p t n -> p n t")
+                )
+
+        def quantise_y(g):
+            codes = codes_pool.tile([P, POINTS], U32, name="y_codes", align_bytes=64)
+            scales = codes_pool.tile([P, POINTS], U8, name="y_scales", align_bytes=64)
+            nc.vector.quantize_mx(
+                out=codes[:].bitcast(FP8X4),
+                scales=scales[:],
+                in_=y_grouped[g][:].rearrange("p n t -> p (n t)"),
+            )
+            y_codes[g] = codes
+            y_scales[g] = scales
+
+        def second_product(g, c_tiles):
+            words = w_words[g // CHUNK_ROUNDS]
+            for c in c_tiles:
+                nc.tensor.matmul_mx(
+                    out=acc[c][:],
+                    lhsT=words[:, g % CHUNK_ROUNDS, c * P : (c + 1) * P].bitcast(FP8X4),
+                    lhsT_scale=w_planes[4 * (g % PLANES) : P, g // PLANES, c * P : (c + 1) * P],
+                    rhs=y_codes[g][:].bitcast(FP8X4),
+                    rhs_scale=y_scales[g][:],
+                    start=(g == 0),
+                    stop=(g == ROUNDS - 1),
+                )
+
+        regroup_g(0)
+        nc.vector.quantize_mx(
+            out=a_codes[:].bitcast(FP8X4), scales=a_scales[:], in_=a_grouped[:].rearrange("p n t -> p (n t)")
+        )
+        for s in range(-3, ROUNDS):
+            if 0 <= s + 1 < ROUNDS:
+                quantise_y(s + 1)
+            if s + 3 < ROUNDS:
+                quantise_g(s + 3)
+            if s + 4 < ROUNDS:
+                regroup_g(s + 4)
+            if s + 4 == ROUNDS:
+                fold_batch_norm()
+            for h in range(2):
+                if 0 <= s + 2 < ROUNDS:
+                    first_product(s + 2, range(h * POINT_BLOCKS // 2, (h + 1) * POINT_BLOCKS // 2))
+                if s >= 0:
+                    second_product(s, range(h * C_TILES // 2, (h + 1) * C_TILES // 2))
+            if s + 2 == ROUNDS - 1:
+                shift_x()
+
+        result = keep.tile([P, C_TILES, POINTS], F32)
+        for c in range(C_TILES):
+            nc.vector.scalar_tensor_tensor(
+                out=result[:, c, :], in0=acc[c][:], scalar=bn_scale[:, c : c + 1], in1=x_shifted[:, c, :],
+                op0=ALU.mult, op1=ALU.add,
+            )
+            nc.sync.dma_start(out=out[0][c * P : (c + 1) * P, :], in_=result[:, c, :])

@@ -23,6 +23,8 @@ EPS = 1e-5
 ROUNDS = INNER // K_PASS
 POINT_BLOCKS = POINTS // P
 C_TILES = CHANNELS // P
+STREAM_TILES = C_TILES - 1
+Y_BANKS = 8 - STREAM_TILES
 CHUNK_ROUNDS = 2
 CHUNKS = ROUNDS // CHUNK_ROUNDS
 PLANES = 4
@@ -43,7 +45,7 @@ def tile_sgcam_pb_k_kernel(
         grouped_pool = ctx.enter_context(tc.tile_pool(name="grouped_pool", bufs=2))
         codes_pool = ctx.enter_context(tc.tile_pool(name="codes_pool", bufs=3))
         acc_pool = ctx.enter_context(tc.psum_pool(name="acc_pool", bufs=1))
-        bank_pool = ctx.enter_context(tc.psum_pool(name="bank_pool", bufs=2))
+        bank_pool = ctx.enter_context(tc.psum_pool(name="bank_pool", bufs=Y_BANKS))
         ctx.enter_context(tc.manual_schedule())
 
         w_planes = keep.tile([P, ROUNDS // PLANES, CHANNELS], U8, align_bytes=64)
@@ -63,13 +65,15 @@ def tile_sgcam_pb_k_kernel(
         g_raw = []
         w_words = []
 
-        def load_g(k):
+        def load_g(k, pieces):
             width = CHUNK_ROUNDS * K_PASS
             raw = g_pool.tile([P, PACK, width], BF16, name="g_raw")
-            nc.sync.dma_start(
-                out=raw[:],
-                in_=g_x[0][:, k * width : (k + 1) * width].rearrange("(p j) c -> p j c", j=PACK),
-            )
+            for i in range(pieces):
+                cols = slice(i * width // pieces, (i + 1) * width // pieces)
+                nc.sync.dma_start(
+                    out=raw[:, :, cols],
+                    in_=g_x[0][:, k * width : (k + 1) * width][:, cols].rearrange("(p j) c -> p j c", j=PACK),
+                )
             g_raw.append(raw)
 
         def load_w_planes(s):
@@ -89,14 +93,14 @@ def tile_sgcam_pb_k_kernel(
             )
             w_words.append(words)
 
-        load_g(0)
-        load_g(1)
+        load_g(0, CHUNK_ROUNDS)
+        load_g(1, 1)
         for k in range(CHUNKS):
             if (k * CHUNK_ROUNDS) % PLANES == 0:
                 load_w_planes(k * CHUNK_ROUNDS // PLANES)
             load_w(k)
             if k + 2 < CHUNKS:
-                load_g(k + 2)
+                load_g(k + 2, 1)
         x_rows = keep.tile([P, C_TILES, POINTS], BF16)
         nc.sync.dma_start(out=x_rows[:], in_=x[0].rearrange("(c p) n -> p c n", p=P))
 
@@ -156,10 +160,10 @@ def tile_sgcam_pb_k_kernel(
         g_codes = {}
         g_scales = {}
         y_grouped = {}
-        y_codes = {}
-        y_scales = {}
+        y_codes = keep.tile([P, ROUNDS, POINTS], U32, align_bytes=64)
+        y_scales = keep.tile([P, ROUNDS, POINTS], U8, align_bytes=64)
         acc = []
-        for c in range(C_TILES):
+        for c in range(STREAM_TILES):
             acc_c = acc_pool.tile([P, POINTS], F32, name="acc%d" % c)
             acc.append(acc_c)
 
@@ -184,49 +188,47 @@ def tile_sgcam_pb_k_kernel(
             g_codes[g] = codes
             g_scales[g] = scales
 
-        def first_product(g, blocks):
-            if g not in y_grouped:
+        def first_product(g, b):
+            if b == 0:
                 grouped = grouped_pool.tile([P, POINTS, PACK], BF16, name="y_grouped", align_bytes=64)
                 y_grouped[g] = grouped
-            for b in blocks:
-                y_bank = bank_pool.tile([P, PACK, P], F32, name="y_bank", tag="bank")
-                for t in range(PACK):
-                    nc.tensor.matmul_mx(
-                        out=y_bank[:, t, :],
-                        lhsT=g_codes[g][:, t * P : (t + 1) * P].bitcast(FP8X4),
-                        lhsT_scale=g_scales[g][:, t * P : (t + 1) * P],
-                        rhs=a_codes[:, b * P : (b + 1) * P].bitcast(FP8X4),
-                        rhs_scale=a_scales[:, b * P : (b + 1) * P],
-                        start=True,
-                        stop=True,
-                    )
-                nc.scalar.copy(
-                    out=y_grouped[g][:, b * P : (b + 1) * P, :], in_=y_bank[:].rearrange("p t n -> p n t")
+            y_bank = bank_pool.tile([P, PACK, P], F32, name="y_bank", tag="bank")
+            for t in range(PACK):
+                nc.tensor.matmul_mx(
+                    out=y_bank[:, t, :],
+                    lhsT=g_codes[g][:, t * P : (t + 1) * P].bitcast(FP8X4),
+                    lhsT_scale=g_scales[g][:, t * P : (t + 1) * P],
+                    rhs=a_codes[:, b * P : (b + 1) * P].bitcast(FP8X4),
+                    rhs_scale=a_scales[:, b * P : (b + 1) * P],
+                    start=True,
+                    stop=True,
                 )
+            nc.scalar.copy(out=y_grouped[g][:, b * P : (b + 1) * P, :], in_=y_bank[:].rearrange("p t n -> p n t"))
 
         def quantise_y(g):
-            codes = codes_pool.tile([P, POINTS], U32, name="y_codes", align_bytes=64)
-            scales = codes_pool.tile([P, POINTS], U8, name="y_scales", align_bytes=64)
             nc.vector.quantize_mx(
-                out=codes[:].bitcast(FP8X4),
-                scales=scales[:],
+                out=y_codes[:, g, :].bitcast(FP8X4),
+                scales=y_scales[:, g, :],
                 in_=y_grouped[g][:].rearrange("p n t -> p (n t)"),
             )
-            y_codes[g] = codes
-            y_scales[g] = scales
 
-        def second_product(g, c_tiles):
-            words = w_words[g // CHUNK_ROUNDS]
-            for c in c_tiles:
-                nc.tensor.matmul_mx(
-                    out=acc[c][:],
-                    lhsT=words[:, g % CHUNK_ROUNDS, c * P : (c + 1) * P].bitcast(FP8X4),
-                    lhsT_scale=w_planes[4 * (g % PLANES) : P, g // PLANES, c * P : (c + 1) * P],
-                    rhs=y_codes[g][:].bitcast(FP8X4),
-                    rhs_scale=y_scales[g][:],
-                    start=(g == 0),
-                    stop=(g == ROUNDS - 1),
-                )
+        def second_product(g, c):
+            nc.tensor.matmul_mx(
+                out=acc[c][:],
+                lhsT=w_words[g // CHUNK_ROUNDS][:, g % CHUNK_ROUNDS, c * P : (c + 1) * P].bitcast(FP8X4),
+                lhsT_scale=w_planes[4 * (g % PLANES) : P, g // PLANES, c * P : (c + 1) * P],
+                rhs=y_codes[:, g, :].bitcast(FP8X4),
+                rhs_scale=y_scales[:, g, :],
+                start=(g == 0),
+                stop=(g == ROUNDS - 1),
+            )
+
+        def finish(c):
+            nc.vector.scalar_tensor_tensor(
+                out=x_shifted[:, c, :], in0=acc[c][:], scalar=bn_scale[:, c : c + 1], in1=x_shifted[:, c, :],
+                op0=ALU.mult, op1=ALU.add,
+            )
+            nc.sync.dma_start(out=out[0][c * P : (c + 1) * P, :], in_=x_shifted[:, c, :])
 
         regroup_g(0)
         nc.vector.quantize_mx(
@@ -241,18 +243,17 @@ def tile_sgcam_pb_k_kernel(
                 regroup_g(s + 4)
             if s + 4 == ROUNDS:
                 fold_batch_norm()
-            for h in range(2):
-                if 0 <= s + 2 < ROUNDS:
-                    first_product(s + 2, range(h * POINT_BLOCKS // 2, (h + 1) * POINT_BLOCKS // 2))
+            for i in range(STREAM_TILES):
+                if i < POINT_BLOCKS and 0 <= s + 2 < ROUNDS:
+                    first_product(s + 2, i)
                 if s >= 0:
-                    second_product(s, range(h * C_TILES // 2, (h + 1) * C_TILES // 2))
+                    second_product(s, i)
             if s + 2 == ROUNDS - 1:
                 shift_x()
 
-        result = keep.tile([P, C_TILES, POINTS], F32)
+        last_acc = bank_pool.tile([P, POINTS], F32, name="last_acc", tag="bank")
+        acc.append(last_acc)
+        for g in range(ROUNDS):
+            second_product(g, STREAM_TILES)
         for c in range(C_TILES):
-            nc.vector.scalar_tensor_tensor(
-                out=result[:, c, :], in0=acc[c][:], scalar=bn_scale[:, c : c + 1], in1=x_shifted[:, c, :],
-                op0=ALU.mult, op1=ALU.add,
-            )
-            nc.sync.dma_start(out=out[0][c * P : (c + 1) * P, :], in_=result[:, c, :])
+            finish(c)

@@ -30,6 +30,7 @@ CHUNKS = ROUNDS // CHUNK_ROUNDS
 PLANES = 4
 QUADRANTS = 4
 VECTORS = 5
+RUN = 4
 
 FLOPS = 2 * POINTS * POINTS * INNER + 2 * CHANNELS * INNER * POINTS
 
@@ -203,7 +204,10 @@ def tile_sgcam_pb_k_kernel(
                     start=True,
                     stop=True,
                 )
-            nc.scalar.copy(out=y_grouped[g][:, b * P : (b + 1) * P, :], in_=y_bank[:].rearrange("p t n -> p n t"))
+            nc.scalar.copy(
+                out=y_grouped[g][:, b * P : (b + 1) * P, :].rearrange("p (c i) t -> p c t i", i=RUN),
+                in_=y_bank[:].rearrange("p t (c i) -> p c t i", i=RUN),
+            )
 
         def quantise_y(g):
             nc.vector.quantize_mx(

@@ -30,7 +30,6 @@ CHUNKS = ROUNDS // CHUNK_ROUNDS
 PLANES = 4
 QUADRANTS = 4
 VECTORS = 5
-RUN = 4
 
 FLOPS = 2 * POINTS * POINTS * INNER + 2 * CHANNELS * INNER * POINTS
 
@@ -61,21 +60,18 @@ def tile_sgcam_pb_k_kernel(
         make_identity(nc, ident_bf16[:])
 
         a_rows = keep.tile([P, POINT_BLOCKS, POINTS], BF16)
-        nc.sync.dma_start(out=a_rows[:], in_=affinity[0].rearrange("(b p) m -> p b m", p=P))
-
         g_raw = []
+        for k in range(CHUNKS):
+            raw = g_pool.tile([P, PACK, CHUNK_ROUNDS * K_PASS], BF16, name="g_raw")
+            g_raw.append(raw)
         w_words = []
 
-        def load_g(k, pieces):
-            width = CHUNK_ROUNDS * K_PASS
-            raw = g_pool.tile([P, PACK, width], BF16, name="g_raw")
-            for i in range(pieces):
-                cols = slice(i * width // pieces, (i + 1) * width // pieces)
-                nc.sync.dma_start(
-                    out=raw[:, :, cols],
-                    in_=g_x[0][:, k * width : (k + 1) * width][:, cols].rearrange("(p j) c -> p j c", j=PACK),
-                )
-            g_raw.append(raw)
+        def load_g(g, rounds):
+            first = (g % CHUNK_ROUNDS) * K_PASS
+            nc.sync.dma_start(
+                out=g_raw[g // CHUNK_ROUNDS][:, :, first : first + rounds * K_PASS],
+                in_=g_x[0][:, g * K_PASS : (g + rounds) * K_PASS].rearrange("(p j) c -> p j c", j=PACK),
+            )
 
         def load_w_planes(s):
             for quad in range(QUADRANTS):
@@ -94,63 +90,64 @@ def tile_sgcam_pb_k_kernel(
             )
             w_words.append(words)
 
-        load_g(0, CHUNK_ROUNDS)
-        load_g(1, 1)
+        load_g(0, 1)
+        for b in range(POINT_BLOCKS):
+            nc.sync.dma_start(out=a_rows[:, b, :], in_=affinity[0][b * P : (b + 1) * P, :])
+        for g in range(1, 2 * CHUNK_ROUNDS):
+            load_g(g, 1)
         for k in range(CHUNKS):
             if (k * CHUNK_ROUNDS) % PLANES == 0:
                 load_w_planes(k * CHUNK_ROUNDS // PLANES)
             load_w(k)
             if k + 2 < CHUNKS:
-                load_g(k + 2, 1)
+                load_g((k + 2) * CHUNK_ROUNDS, CHUNK_ROUNDS)
+        for v, vec in enumerate((w_b, bn_gamma, bn_beta, bn_mean, bn_var)):
+            nc.sync.dma_start(
+                out=vec_rows[C_TILES * v : C_TILES * (v + 1), :], in_=vec.rearrange("(c p) -> c p", p=P)
+            )
         x_rows = keep.tile([P, C_TILES, POINTS], BF16)
         nc.sync.dma_start(out=x_rows[:], in_=x[0].rearrange("(c p) n -> p c n", p=P))
 
-        for v, vec in enumerate((w_b, bn_gamma, bn_beta, bn_mean, bn_var)):
-            nc.scalar.dma_start(
-                out=vec_rows[C_TILES * v : C_TILES * (v + 1), :], in_=vec.rearrange("(c p) -> c p", p=P)
-            )
         warm = keep.tile([P, 1], F32)
         nc.scalar.sqrt(out=warm[:], in_=eps_col[:])
 
         a_grouped = keep.tile([P, POINTS, PACK], BF16, align_bytes=64)
         a_grouped_words = a_grouped[:].rearrange("p n t -> p (n t)").bitcast(F32).rearrange("p (n u) -> p n u", u=2)
-        half_points = POINTS // 2
-        for h in range(2):
-            a_bank = bank_pool.tile([P, 2, half_points], F32, name="a_bank", tag="bank")
+        for b in range(POINT_BLOCKS):
+            a_bank = bank_pool.tile([P, 2, P], F32, name="a_bank", tag="bank")
             for u in range(2):
-                for i in range(half_points // P):
-                    b = h * (half_points // P) + i
-                    nc.tensor.transpose(
-                        a_bank[:, u, i * P : (i + 1) * P],
-                        a_rows[:, b, :].bitcast(F32)[:, u : POINTS // 2 : 2],
-                        ident_f32[:],
-                    )
+                nc.tensor.transpose(
+                    a_bank[:, u, :], a_rows[:, b, :].bitcast(F32)[:, u : POINTS // 2 : 2], ident_f32[:]
+                )
             nc.scalar.copy(
-                out=a_grouped_words[:, h * half_points : (h + 1) * half_points, :],
-                in_=a_bank[:].rearrange("p u n -> p n u"),
+                out=a_grouped_words[:, b * P : (b + 1) * P, :], in_=a_bank[:].rearrange("p u n -> p n u")
             )
         a_codes = keep.tile([P, POINTS], U32, align_bytes=64)
         a_scales = keep.tile([P, POINTS], U8, align_bytes=64)
 
-        vec_bank = bank_pool.tile([P, P], BF16, name="vec_bank", tag="bank")
-        nc.tensor.transpose(vec_bank[:], vec_rows[:], ident_bf16[:])
+        def quantise_a(b):
+            nc.vector.quantize_mx(
+                out=a_codes[:, b * P : (b + 1) * P].bitcast(FP8X4),
+                scales=a_scales[:, b * P : (b + 1) * P],
+                in_=a_grouped[:, b * P : (b + 1) * P, :].rearrange("p n t -> p (n t)"),
+            )
+
         vec_cols = keep.tile([P, VECTORS, C_TILES], F32)
-        nc.scalar.copy(out=vec_cols[:].rearrange("p v c -> p (v c)"), in_=vec_bank[:, 0 : VECTORS * C_TILES])
         std = keep.tile([P, C_TILES], F32)
-        nc.scalar.activation(out=std[:], in_=vec_cols[:, 4, :], func=ACT.Sqrt, bias=eps_col[:, 0:1], scale=1.0)
         bn_scale = keep.tile([P, C_TILES], F32)
         bn_shift = keep.tile([P, C_TILES], F32)
+        x_shifted = keep.tile([P, C_TILES, POINTS], F32)
 
-        def fold_batch_norm():
+        def prepare_batch_norm():
+            vec_bank = bank_pool.tile([P, P], BF16, name="vec_bank", tag="bank")
+            nc.tensor.transpose(vec_bank[:], vec_rows[:], ident_bf16[:])
+            nc.scalar.copy(out=vec_cols[:].rearrange("p v c -> p (v c)"), in_=vec_bank[:, 0 : VECTORS * C_TILES])
+            nc.scalar.activation(out=std[:], in_=vec_cols[:, 4, :], func=ACT.Sqrt, bias=eps_col[:, 0:1], scale=1.0)
             nc.vector.reciprocal(out=bn_scale[:], in_=std[:])
             nc.vector.tensor_sub(out=bn_shift[:], in0=vec_cols[:, 0, :], in1=vec_cols[:, 3, :])
             nc.vector.tensor_mul(out=bn_scale[:], in0=bn_scale[:], in1=vec_cols[:, 1, :])
             nc.vector.tensor_mul(out=bn_shift[:], in0=bn_shift[:], in1=bn_scale[:])
             nc.vector.tensor_add(out=bn_shift[:], in0=bn_shift[:], in1=vec_cols[:, 2, :])
-
-        x_shifted = keep.tile([P, C_TILES, POINTS], F32)
-
-        def shift_x():
             for c in range(C_TILES):
                 nc.scalar.activation(
                     out=x_shifted[:, c, :], in_=x_rows[:, c, :], func=ACT.Identity,
@@ -204,10 +201,7 @@ def tile_sgcam_pb_k_kernel(
                     start=True,
                     stop=True,
                 )
-            nc.scalar.copy(
-                out=y_grouped[g][:, b * P : (b + 1) * P, :].rearrange("p (c i) t -> p c t i", i=RUN),
-                in_=y_bank[:].rearrange("p t (c i) -> p c t i", i=RUN),
-            )
+            nc.scalar.copy(out=y_grouped[g][:, b * P : (b + 1) * P, :], in_=y_bank[:].rearrange("p t n -> p n t"))
 
         def quantise_y(g):
             nc.vector.quantize_mx(
@@ -216,48 +210,51 @@ def tile_sgcam_pb_k_kernel(
                 in_=y_grouped[g][:].rearrange("p n t -> p (n t)"),
             )
 
-        def second_product(g, c):
+        def second_product(g, c, points, group):
             nc.tensor.matmul_mx(
-                out=acc[c][:],
+                out=group[:],
                 lhsT=w_words[g // CHUNK_ROUNDS][:, g % CHUNK_ROUNDS, c * P : (c + 1) * P].bitcast(FP8X4),
                 lhsT_scale=w_planes[4 * (g % PLANES) : P, g // PLANES, c * P : (c + 1) * P],
-                rhs=y_codes[:, g, :].bitcast(FP8X4),
-                rhs_scale=y_scales[:, g, :],
+                rhs=y_codes[:, g, points].bitcast(FP8X4),
+                rhs_scale=y_scales[:, g, points],
                 start=(g == 0),
                 stop=(g == ROUNDS - 1),
             )
 
-        def finish(c):
+        def finish(c, points, group):
             nc.vector.scalar_tensor_tensor(
-                out=x_shifted[:, c, :], in0=acc[c][:], scalar=bn_scale[:, c : c + 1], in1=x_shifted[:, c, :],
-                op0=ALU.mult, op1=ALU.add,
+                out=x_shifted[:, c, points], in0=group[:], scalar=bn_scale[:, c : c + 1],
+                in1=x_shifted[:, c, points], op0=ALU.mult, op1=ALU.add,
             )
-            nc.sync.dma_start(out=out[0][c * P : (c + 1) * P, :], in_=x_shifted[:, c, :])
+            nc.sync.dma_start(out=out[0][c * P : (c + 1) * P, points], in_=x_shifted[:, c, points])
 
+        all_points = slice(0, POINTS)
         regroup_g(0)
-        nc.vector.quantize_mx(
-            out=a_codes[:].bitcast(FP8X4), scales=a_scales[:], in_=a_grouped[:].rearrange("p n t -> p (n t)")
-        )
-        for s in range(-3, ROUNDS):
+        quantise_a(0)
+        quantise_g(0)
+        for b in range(1, POINT_BLOCKS):
+            quantise_a(b)
+        regroup_g(1)
+        for s in range(-2, ROUNDS):
             if 0 <= s + 1 < ROUNDS:
                 quantise_y(s + 1)
             if s + 3 < ROUNDS:
                 quantise_g(s + 3)
             if s + 4 < ROUNDS:
                 regroup_g(s + 4)
-            if s + 4 == ROUNDS:
-                fold_batch_norm()
+            if s + 1 == ROUNDS - 1:
+                prepare_batch_norm()
             for i in range(STREAM_TILES):
-                if i < POINT_BLOCKS and 0 <= s + 2 < ROUNDS:
-                    first_product(s + 2, i)
                 if s >= 0:
-                    second_product(s, i)
-            if s + 2 == ROUNDS - 1:
-                shift_x()
+                    second_product(s, i, all_points, acc[i])
+                if i < POINT_BLOCKS and s + 2 < ROUNDS:
+                    first_product(s + 2, i)
+        for c in range(STREAM_TILES):
+            finish(c, all_points, acc[c])
 
-        last_acc = bank_pool.tile([P, POINTS], F32, name="last_acc", tag="bank")
-        acc.append(last_acc)
-        for g in range(ROUNDS):
-            second_product(g, STREAM_TILES)
-        for c in range(C_TILES):
-            finish(c)
+        for h in range(2):
+            half = slice(h * POINTS // 2, (h + 1) * POINTS // 2)
+            last_acc = bank_pool.tile([P, POINTS // 2], F32, name="last_acc", tag="bank")
+            for g in range(ROUNDS):
+                second_product(g, STREAM_TILES, half, last_acc)
+            finish(STREAM_TILES, half, last_acc)

@@ -27,6 +27,7 @@ STREAM_TILES = C_TILES - 1
 Y_BANKS = 8 - STREAM_TILES
 CHUNK_ROUNDS = 2
 CHUNKS = ROUNDS // CHUNK_ROUNDS
+SINGLE_ROUNDS = 2 * CHUNK_ROUNDS
 PLANES = 4
 QUADRANTS = 4
 VECTORS = 5
@@ -40,7 +41,7 @@ def tile_sgcam_pb_k_kernel(
     nc = tc.nc
     with ExitStack() as ctx:
         keep = ctx.enter_context(tc.tile_pool(name="keep", bufs=1))
-        g_pool = ctx.enter_context(tc.tile_pool(name="g_pool", bufs=CHUNKS))
+        g_pool = ctx.enter_context(tc.tile_pool(name="g_pool", bufs=CHUNKS - SINGLE_ROUNDS // CHUNK_ROUNDS))
         w_pool = ctx.enter_context(tc.tile_pool(name="w_pool", bufs=CHUNKS))
         grouped_pool = ctx.enter_context(tc.tile_pool(name="grouped_pool", bufs=2))
         codes_pool = ctx.enter_context(tc.tile_pool(name="codes_pool", bufs=3))
@@ -61,15 +62,19 @@ def tile_sgcam_pb_k_kernel(
 
         a_rows = keep.tile([P, POINT_BLOCKS, POINTS], BF16)
         g_raw = []
-        for k in range(CHUNKS):
+        for g in range(SINGLE_ROUNDS):
+            raw = keep.tile([P, PACK, K_PASS], BF16, name="g_single%d" % g)
+            g_raw.append((raw, 0))
+        for k in range(SINGLE_ROUNDS // CHUNK_ROUNDS, CHUNKS):
             raw = g_pool.tile([P, PACK, CHUNK_ROUNDS * K_PASS], BF16, name="g_raw")
-            g_raw.append(raw)
+            for i in range(CHUNK_ROUNDS):
+                g_raw.append((raw, i * K_PASS))
         w_words = []
 
         def load_g(g, rounds):
-            first = (g % CHUNK_ROUNDS) * K_PASS
+            raw, first = g_raw[g]
             nc.sync.dma_start(
-                out=g_raw[g // CHUNK_ROUNDS][:, :, first : first + rounds * K_PASS],
+                out=raw[:, :, first : first + rounds * K_PASS],
                 in_=g_x[0][:, g * K_PASS : (g + rounds) * K_PASS].rearrange("(p j) c -> p j c", j=PACK),
             )
 
@@ -93,7 +98,7 @@ def tile_sgcam_pb_k_kernel(
         load_g(0, 1)
         for b in range(POINT_BLOCKS):
             nc.sync.dma_start(out=a_rows[:, b, :], in_=affinity[0][b * P : (b + 1) * P, :])
-        for g in range(1, 2 * CHUNK_ROUNDS):
+        for g in range(1, SINGLE_ROUNDS):
             load_g(g, 1)
         for k in range(CHUNKS):
             if (k * CHUNK_ROUNDS) % PLANES == 0:
@@ -166,8 +171,7 @@ def tile_sgcam_pb_k_kernel(
             acc.append(acc_c)
 
         def regroup_g(g):
-            raw = g_raw[g // CHUNK_ROUNDS]
-            first = (g % CHUNK_ROUNDS) * K_PASS
+            raw, first = g_raw[g]
             grouped = grouped_pool.tile([P, PACK, P, PACK], BF16, name="g_grouped", align_bytes=64)
             nc.vector.tensor_copy(
                 out=grouped[:].rearrange("p t q j -> p q j t"),

@@ -27,6 +27,8 @@ STREAM_TILES = C_TILES - 1
 Y_BANKS = 8 - STREAM_TILES
 CHUNK_ROUNDS = 2
 CHUNKS = ROUNDS // CHUNK_ROUNDS
+EARLY_PASSES = 4
+FIRST_STEP_LAG = 2
 SINGLE_ROUNDS = 2 * CHUNK_ROUNDS
 PLANES = 4
 QUADRANTS = 4
@@ -51,14 +53,10 @@ def tile_sgcam_pb_k_kernel(
 
         w_planes = keep.tile([P, ROUNDS // PLANES, CHANNELS], U8, align_bytes=64)
         nc.vector.memset(w_planes[:].rearrange("p s n -> p (s n)").bitcast(I32), 0)
-        vec_rows = keep.tile([P, P], BF16)
-        nc.vector.memset(vec_rows[:], 0.0)
         eps_col = keep.tile([P, 1], F32)
         nc.vector.memset(eps_col[:], EPS)
         ident_f32 = keep.tile([P, P], F32)
         make_identity(nc, ident_f32[:])
-        ident_bf16 = keep.tile([P, P], BF16)
-        make_identity(nc, ident_bf16[:])
 
         a_rows = keep.tile([P, POINT_BLOCKS, POINTS], BF16)
         g_raw = []
@@ -106,10 +104,12 @@ def tile_sgcam_pb_k_kernel(
             load_w(k)
             if k + 2 < CHUNKS:
                 load_g((k + 2) * CHUNK_ROUNDS, CHUNK_ROUNDS)
-        for v, vec in enumerate((w_b, bn_gamma, bn_beta, bn_mean, bn_var)):
-            nc.sync.dma_start(
-                out=vec_rows[C_TILES * v : C_TILES * (v + 1), :], in_=vec.rearrange("(c p) -> c p", p=P)
-            )
+        vec_cols = keep.tile([P, VECTORS, 8, 2], BF16)
+        with nc.allow_non_contiguous_dma(reason="five vectors of 768 values, one value to a partition"):
+            for v, vec in enumerate((w_b, bn_gamma, bn_beta, bn_mean, bn_var)):
+                nc.sync.dma_start(
+                    out=vec_cols[:, v, 0:C_TILES, 0:1], in_=vec.rearrange("(c p one) -> p c one", p=P, one=1)
+                )
         x_rows = keep.tile([P, C_TILES, POINTS], BF16)
         nc.sync.dma_start(out=x_rows[:], in_=x[0].rearrange("(c p) n -> p c n", p=P))
 
@@ -137,22 +137,20 @@ def tile_sgcam_pb_k_kernel(
                 in_=a_grouped[:, b * P : (b + 1) * P, :].rearrange("p n t -> p (n t)"),
             )
 
-        vec_cols = keep.tile([P, VECTORS, C_TILES], F32)
         std = keep.tile([P, C_TILES], F32)
         bn_scale = keep.tile([P, C_TILES], F32)
         bn_shift = keep.tile([P, C_TILES], F32)
         x_shifted = keep.tile([P, C_TILES, POINTS], F32)
 
         def prepare_batch_norm():
-            vec_bank = bank_pool.tile([P, P], BF16, name="vec_bank", tag="bank")
-            nc.tensor.transpose(vec_bank[:], vec_rows[:], ident_bf16[:])
-            nc.scalar.copy(out=vec_cols[:].rearrange("p v c -> p (v c)"), in_=vec_bank[:, 0 : VECTORS * C_TILES])
-            nc.scalar.activation(out=std[:], in_=vec_cols[:, 4, :], func=ACT.Sqrt, bias=eps_col[:, 0:1], scale=1.0)
+            nc.scalar.activation(
+                out=std[:], in_=vec_cols[:, 4, 0:C_TILES, 0], func=ACT.Sqrt, bias=eps_col[:, 0:1], scale=1.0
+            )
             nc.vector.reciprocal(out=bn_scale[:], in_=std[:])
-            nc.vector.tensor_sub(out=bn_shift[:], in0=vec_cols[:, 0, :], in1=vec_cols[:, 3, :])
-            nc.vector.tensor_mul(out=bn_scale[:], in0=bn_scale[:], in1=vec_cols[:, 1, :])
+            nc.vector.tensor_sub(out=bn_shift[:], in0=vec_cols[:, 0, 0:C_TILES, 0], in1=vec_cols[:, 3, 0:C_TILES, 0])
+            nc.vector.tensor_mul(out=bn_scale[:], in0=bn_scale[:], in1=vec_cols[:, 1, 0:C_TILES, 0])
             nc.vector.tensor_mul(out=bn_shift[:], in0=bn_shift[:], in1=bn_scale[:])
-            nc.vector.tensor_add(out=bn_shift[:], in0=bn_shift[:], in1=vec_cols[:, 2, :])
+            nc.vector.tensor_add(out=bn_shift[:], in0=bn_shift[:], in1=vec_cols[:, 2, 0:C_TILES, 0])
             for c in range(C_TILES):
                 nc.scalar.activation(
                     out=x_shifted[:, c, :], in_=x_rows[:, c, :], func=ACT.Identity,
@@ -233,6 +231,13 @@ def tile_sgcam_pb_k_kernel(
             nc.sync.dma_start(out=out[0][c * P : (c + 1) * P, points], in_=x_shifted[:, c, points])
 
         all_points = slice(0, POINTS)
+        halves = [slice(0, POINTS // 2), slice(POINTS // 2, POINTS)]
+        last_acc = []
+
+        def open_last_acc():
+            group = bank_pool.tile([P, POINTS // 2], F32, name="last_acc", tag="bank")
+            last_acc.append(group)
+
         regroup_g(0)
         quantise_a(0)
         quantise_g(0)
@@ -248,17 +253,22 @@ def tile_sgcam_pb_k_kernel(
                 regroup_g(s + 4)
             if s + 1 == ROUNDS - 1:
                 prepare_batch_norm()
-            for i in range(STREAM_TILES):
-                if s >= 0:
+            lag = FIRST_STEP_LAG if s == 0 else 0
+            if s == ROUNDS - 1:
+                open_last_acc()
+                for g in range(EARLY_PASSES):
+                    second_product(g, STREAM_TILES, halves[0], last_acc[0])
+            for i in range(STREAM_TILES + lag):
+                if s >= 0 and i < STREAM_TILES:
                     second_product(s, i, all_points, acc[i])
-                if i < POINT_BLOCKS and s + 2 < ROUNDS:
-                    first_product(s + 2, i)
+                if 0 <= i - lag < POINT_BLOCKS and s + 2 < ROUNDS:
+                    first_product(s + 2, i - lag)
         for c in range(STREAM_TILES):
             finish(c, all_points, acc[c])
 
         for h in range(2):
-            half = slice(h * POINTS // 2, (h + 1) * POINTS // 2)
-            last_acc = bank_pool.tile([P, POINTS // 2], F32, name="last_acc", tag="bank")
-            for g in range(ROUNDS):
-                second_product(g, STREAM_TILES, half, last_acc)
-            finish(STREAM_TILES, half, last_acc)
+            if h > 0:
+                open_last_acc()
+            for g in range(EARLY_PASSES if h == 0 else 0, ROUNDS):
+                second_product(g, STREAM_TILES, halves[h], last_acc[h])
+            finish(STREAM_TILES, halves[h], last_acc[h])

@@ -29,7 +29,7 @@ CHUNK_ROUNDS = 2
 CHUNKS = ROUNDS // CHUNK_ROUNDS
 EARLY_PASSES = 4
 FIRST_STEP_LAG = 2
-SINGLE_ROUNDS = 2 * CHUNK_ROUNDS
+SINGLE_ROUNDS = 4 * CHUNK_ROUNDS
 PLANES = 4
 QUADRANTS = 4
 VECTORS = 5
@@ -68,6 +68,9 @@ def tile_sgcam_pb_k_kernel(
             for i in range(CHUNK_ROUNDS):
                 g_raw.append((raw, i * K_PASS))
         w_words = []
+        for k in range(CHUNKS):
+            words = w_pool.tile([P, CHUNK_ROUNDS, CHANNELS], U32, name="w_words", align_bytes=64)
+            w_words.append(words)
 
         def load_g(g, rounds):
             raw, first = g_raw[g]
@@ -83,27 +86,32 @@ def tile_sgcam_pb_k_kernel(
                     in_=w_w_scales[PLANES * s : PLANES * (s + 1), 4 * quad : 4 * quad + 4, :].bitcast(I32),
                 )
 
-        def load_w(k):
-            words = w_pool.tile([P, CHUNK_ROUNDS, CHANNELS], U32, name="w_words", align_bytes=64)
+        def load_w(g, rounds, c_from, c_to):
+            i = g % CHUNK_ROUNDS
             nc.sync.dma_start(
-                out=words[:].bitcast(I32),
-                in_=w_w_words[CHUNK_ROUNDS * k : CHUNK_ROUNDS * (k + 1)]
-                .rearrange("g p n t -> p g (n t)")
+                out=w_words[g // CHUNK_ROUNDS][:, i : i + rounds, c_from * P : c_to * P].bitcast(I32),
+                in_=w_w_words[g : g + rounds]
+                .rearrange("g p n t -> p g (n t)")[:, :, c_from * P * PACK : c_to * P * PACK]
                 .bitcast(I32),
             )
-            w_words.append(words)
 
         load_g(0, 1)
         for b in range(POINT_BLOCKS):
             nc.sync.dma_start(out=a_rows[:, b, :], in_=affinity[0][b * P : (b + 1) * P, :])
-        for g in range(1, SINGLE_ROUNDS):
-            load_g(g, 1)
-        for k in range(CHUNKS):
-            if (k * CHUNK_ROUNDS) % PLANES == 0:
-                load_w_planes(k * CHUNK_ROUNDS // PLANES)
-            load_w(k)
-            if k + 2 < CHUNKS:
-                load_g((k + 2) * CHUNK_ROUNDS, CHUNK_ROUNDS)
+        load_g(1, 1)
+        load_g(2, 1)
+        for s in range(SINGLE_ROUNDS - 3):
+            if s % PLANES == 0:
+                load_w_planes(s // PLANES)
+            load_w(s, 1, 0, STREAM_TILES)
+            load_g(s + 3, 1)
+        load_w(SINGLE_ROUNDS - 3, 1, 0, STREAM_TILES)
+        for s in range(SINGLE_ROUNDS - 2, ROUNDS, CHUNK_ROUNDS):
+            if s + 2 < ROUNDS:
+                load_g(s + 2, CHUNK_ROUNDS)
+            if s % PLANES == 0:
+                load_w_planes(s // PLANES)
+            load_w(s, CHUNK_ROUNDS, 0, STREAM_TILES if s < SINGLE_ROUNDS else C_TILES)
         vec_cols = keep.tile([P, VECTORS, 8, 2], BF16)
         with nc.allow_non_contiguous_dma(reason="five vectors of 768 values, one value to a partition"):
             for v, vec in enumerate((w_b, bn_gamma, bn_beta, bn_mean, bn_var)):
@@ -112,6 +120,8 @@ def tile_sgcam_pb_k_kernel(
                 )
         x_rows = keep.tile([P, C_TILES, POINTS], BF16)
         nc.sync.dma_start(out=x_rows[:], in_=x[0].rearrange("(c p) n -> p c n", p=P))
+        for s in range(0, SINGLE_ROUNDS, CHUNK_ROUNDS):
+            load_w(s, CHUNK_ROUNDS, STREAM_TILES, C_TILES)
 
         warm = keep.tile([P, 1], F32)
         nc.scalar.sqrt(out=warm[:], in_=eps_col[:])

@@ -263,7 +263,7 @@ def tile_sgcam_pb_k_kernel(
                 regroup_g(s + 4)
             if s + 1 == ROUNDS - 1:
                 prepare_batch_norm()
-            lag = FIRST_STEP_LAG if s == 0 else 0
+            lag = max(0, FIRST_STEP_LAG - s)
             if s == ROUNDS - 1:
                 open_last_acc()
                 for g in range(EARLY_PASSES):

from contextlib import ExitStack

import concourse.mybir as mybir
from concourse.masks import make_identity

F32 = mybir.dt.float32
BF16 = mybir.dt.bfloat16
I32 = mybir.dt.int32
U32 = mybir.dt.uint32
U8 = mybir.dt.uint8
FP8X4 = mybir.dt.float8_e4m3fn_x4
ALU = mybir.AluOpType
ACT = mybir.ActivationFunctionType

P = 128
PACK = 4
K_PASS = P * PACK
POINTS = 512
INNER = 8192
CHANNELS = 768
EPS = 1e-5

ROUNDS = INNER // K_PASS
POINT_BLOCKS = POINTS // P
C_TILES = CHANNELS // P
STREAM_TILES = C_TILES - 1
Y_BANKS = 8 - STREAM_TILES
CHUNK_ROUNDS = 2
CHUNKS = ROUNDS // CHUNK_ROUNDS
EARLY_PASSES = 4
FIRST_STEP_LAG = 2
SINGLE_ROUNDS = 4 * CHUNK_ROUNDS
PLANES = 4
QUADRANTS = 4
VECTORS = 5

FLOPS = 2 * POINTS * POINTS * INNER + 2 * CHANNELS * INNER * POINTS


def tile_sgcam_pb_k_kernel(
    tc, affinity, g_x, w_w_words, w_w_scales, w_b, bn_gamma, bn_beta, bn_mean, bn_var, x, out
):
    nc = tc.nc
    with ExitStack() as ctx:
        keep = ctx.enter_context(tc.tile_pool(name="keep", bufs=1))
        g_pool = ctx.enter_context(tc.tile_pool(name="g_pool", bufs=CHUNKS - SINGLE_ROUNDS // CHUNK_ROUNDS))
        w_pool = ctx.enter_context(tc.tile_pool(name="w_pool", bufs=CHUNKS))
        grouped_pool = ctx.enter_context(tc.tile_pool(name="grouped_pool", bufs=2))
        codes_pool = ctx.enter_context(tc.tile_pool(name="codes_pool", bufs=3))
        acc_pool = ctx.enter_context(tc.psum_pool(name="acc_pool", bufs=1))
        bank_pool = ctx.enter_context(tc.psum_pool(name="bank_pool", bufs=Y_BANKS))
        ctx.enter_context(tc.manual_schedule())

        w_planes = keep.tile([P, ROUNDS // PLANES, CHANNELS], U8, align_bytes=64)
        nc.vector.memset(w_planes[:].rearrange("p s n -> p (s n)").bitcast(I32), 0)
        eps_col = keep.tile([P, 1], F32)
        nc.vector.memset(eps_col[:], EPS)
        ident_f32 = keep.tile([P, P], F32)
        make_identity(nc, ident_f32[:])

        a_rows = keep.tile([P, POINT_BLOCKS, POINTS], BF16)
        g_raw = []
        for g in range(SINGLE_ROUNDS):
            raw = keep.tile([P, PACK, K_PASS], BF16, name="g_single%d" % g)
            g_raw.append((raw, 0))
        for k in range(SINGLE_ROUNDS // CHUNK_ROUNDS, CHUNKS):
            raw = g_pool.tile([P, PACK, CHUNK_ROUNDS * K_PASS], BF16, name="g_raw")
            for i in range(CHUNK_ROUNDS):
                g_raw.append((raw, i * K_PASS))
        w_words = []
        for k in range(CHUNKS):
            words = w_pool.tile([P, CHUNK_ROUNDS, CHANNELS], U32, name="w_words", align_bytes=64)
            w_words.append(words)

        def load_g(g, rounds):
            raw, first = g_raw[g]
            nc.sync.dma_start(
                out=raw[:, :, first : first + rounds * K_PASS],
                in_=g_x[0][:, g * K_PASS : (g + rounds) * K_PASS].rearrange("(p j) c -> p j c", j=PACK),
            )

        def load_w_planes(s):
            for quad in range(QUADRANTS):
                nc.sync.dma_start(
                    out=w_planes[32 * quad : 32 * quad + PLANES * 4, s, :].bitcast(I32),
                    in_=w_w_scales[PLANES * s : PLANES * (s + 1), 4 * quad : 4 * quad + 4, :].bitcast(I32),
                )

        def load_w(g, rounds, c_from, c_to):
            i = g % CHUNK_ROUNDS
            nc.sync.dma_start(
                out=w_words[g // CHUNK_ROUNDS][:, i : i + rounds, c_from * P : c_to * P].bitcast(I32),
                in_=w_w_words[g : g + rounds]
                .rearrange("g p n t -> p g (n t)")[:, :, c_from * P * PACK : c_to * P * PACK]
                .bitcast(I32),
            )

        load_g(0, 1)
        for b in range(POINT_BLOCKS):
            nc.sync.dma_start(out=a_rows[:, b, :], in_=affinity[0][b * P : (b + 1) * P, :])
        load_g(1, 1)
        load_g(2, 1)
        for s in range(SINGLE_ROUNDS - 3):
            if s % PLANES == 0:
                load_w_planes(s // PLANES)
            load_w(s, 1, 0, STREAM_TILES)
            load_g(s + 3, 1)
        load_w(SINGLE_ROUNDS - 3, 1, 0, STREAM_TILES)
        for s in range(SINGLE_ROUNDS - 2, ROUNDS, CHUNK_ROUNDS):
            if s + 2 < ROUNDS:
                load_g(s + 2, CHUNK_ROUNDS)
            if s % PLANES == 0:
                load_w_planes(s // PLANES)
            load_w(s, CHUNK_ROUNDS, 0, STREAM_TILES if s < SINGLE_ROUNDS else C_TILES)
        vec_cols = keep.tile([P, VECTORS, 8, 2], BF16)
        with nc.allow_non_contiguous_dma(reason="five vectors of 768 values, one value to a partition"):
            for v, vec in enumerate((w_b, bn_gamma, bn_beta, bn_mean, bn_var)):
                nc.sync.dma_start(
                    out=vec_cols[:, v, 0:C_TILES, 0:1], in_=vec.rearrange("(c p one) -> p c one", p=P, one=1)
                )
        x_rows = keep.tile([P, C_TILES, POINTS], BF16)
        nc.sync.dma_start(out=x_rows[:], in_=x[0].rearrange("(c p) n -> p c n", p=P))
        for s in range(0, SINGLE_ROUNDS, CHUNK_ROUNDS):
            load_w(s, CHUNK_ROUNDS, STREAM_TILES, C_TILES)

        warm = keep.tile([P, 1], F32)
        nc.scalar.sqrt(out=warm[:], in_=eps_col[:])

        a_grouped = keep.tile([P, POINTS, PACK], BF16, align_bytes=64)
        a_grouped_words = a_grouped[:].rearrange("p n t -> p (n t)").bitcast(F32).rearrange("p (n u) -> p n u", u=2)
        for b in range(POINT_BLOCKS):
            a_bank = bank_pool.tile([P, 2, P], F32, name="a_bank", tag="bank")
            for u in range(2):
                nc.tensor.transpose(
                    a_bank[:, u, :], a_rows[:, b, :].bitcast(F32)[:, u : POINTS // 2 : 2], ident_f32[:]
                )
            nc.scalar.copy(
                out=a_grouped_words[:, b * P : (b + 1) * P, :], in_=a_bank[:].rearrange("p u n -> p n u")
            )
        a_codes = keep.tile([P, POINTS], U32, align_bytes=64)
        a_scales = keep.tile([P, POINTS], U8, align_bytes=64)

        def quantise_a(b):
            nc.vector.quantize_mx(
                out=a_codes[:, b * P : (b + 1) * P].bitcast(FP8X4),
                scales=a_scales[:, b * P : (b + 1) * P],
                in_=a_grouped[:, b * P : (b + 1) * P, :].rearrange("p n t -> p (n t)"),
            )

        std = keep.tile([P, C_TILES], F32)
        bn_scale = keep.tile([P, C_TILES], F32)
        bn_shift = keep.tile([P, C_TILES], F32)
        x_shifted = keep.tile([P, C_TILES, POINTS], F32)

        def prepare_batch_norm():
            nc.scalar.activation(
                out=std[:], in_=vec_cols[:, 4, 0:C_TILES, 0], func=ACT.Sqrt, bias=eps_col[:, 0:1], scale=1.0
            )
            nc.vector.reciprocal(out=bn_scale[:], in_=std[:])
            nc.vector.tensor_sub(out=bn_shift[:], in0=vec_cols[:, 0, 0:C_TILES, 0], in1=vec_cols[:, 3, 0:C_TILES, 0])
            nc.vector.tensor_mul(out=bn_scale[:], in0=bn_scale[:], in1=vec_cols[:, 1, 0:C_TILES, 0])
            nc.vector.tensor_mul(out=bn_shift[:], in0=bn_shift[:], in1=bn_scale[:])
            nc.vector.tensor_add(out=bn_shift[:], in0=bn_shift[:], in1=vec_cols[:, 2, 0:C_TILES, 0])
            for c in range(C_TILES):
                nc.scalar.activation(
                    out=x_shifted[:, c, :], in_=x_rows[:, c, :], func=ACT.Identity,
                    bias=bn_shift[:, c : c + 1], scale=1.0,
                )

        g_grouped = {}
        g_codes = {}
        g_scales = {}
        y_grouped = {}
        y_codes = keep.tile([P, ROUNDS, POINTS], U32, align_bytes=64)
        y_scales = keep.tile([P, ROUNDS, POINTS], U8, align_bytes=64)
        acc = []
        for c in range(STREAM_TILES):
            acc_c = acc_pool.tile([P, POINTS], F32, name="acc%d" % c)
            acc.append(acc_c)

        def regroup_g(g):
            raw, first = g_raw[g]
            grouped = grouped_pool.tile([P, PACK, P, PACK], BF16, name="g_grouped", align_bytes=64)
            nc.vector.tensor_copy(
                out=grouped[:].rearrange("p t q j -> p q j t"),
                in_=raw[:, :, first : first + K_PASS].rearrange("p j (q t) -> p q j t", t=PACK),
            )
            g_grouped[g] = grouped

        def quantise_g(g):
            codes = codes_pool.tile([P, K_PASS], U32, name="g_codes", align_bytes=64)
            scales = codes_pool.tile([P, K_PASS], U8, name="g_scales", align_bytes=64)
            nc.vector.quantize_mx(
                out=codes[:].bitcast(FP8X4),
                scales=scales[:],
                in_=g_grouped[g][:].rearrange("p t q j -> p (t q j)"),
            )
            g_codes[g] = codes
            g_scales[g] = scales

        def first_product(g, b):
            if b == 0:
                grouped = grouped_pool.tile([P, POINTS, PACK], BF16, name="y_grouped", align_bytes=64)
                y_grouped[g] = grouped
            y_bank = bank_pool.tile([P, PACK, P], F32, name="y_bank", tag="bank")
            for t in range(PACK):
                nc.tensor.matmul_mx(
                    out=y_bank[:, t, :],
                    lhsT=g_codes[g][:, t * P : (t + 1) * P].bitcast(FP8X4),
                    lhsT_scale=g_scales[g][:, t * P : (t + 1) * P],
                    rhs=a_codes[:, b * P : (b + 1) * P].bitcast(FP8X4),
                    rhs_scale=a_scales[:, b * P : (b + 1) * P],
                    start=True,
                    stop=True,
                )
            nc.scalar.copy(out=y_grouped[g][:, b * P : (b + 1) * P, :], in_=y_bank[:].rearrange("p t n -> p n t"))

        def quantise_y(g):
            nc.vector.quantize_mx(
                out=y_codes[:, g, :].bitcast(FP8X4),
                scales=y_scales[:, g, :],
                in_=y_grouped[g][:].rearrange("p n t -> p (n t)"),
            )

        def second_product(g, c, points, group):
            nc.tensor.matmul_mx(
                out=group[:],
                lhsT=w_words[g // CHUNK_ROUNDS][:, g % CHUNK_ROUNDS, c * P : (c + 1) * P].bitcast(FP8X4),
                lhsT_scale=w_planes[4 * (g % PLANES) : P, g // PLANES, c * P : (c + 1) * P],
                rhs=y_codes[:, g, points].bitcast(FP8X4),
                rhs_scale=y_scales[:, g, points],
                start=(g == 0),
                stop=(g == ROUNDS - 1),
            )

        def finish(c, points, group):
            nc.vector.scalar_tensor_tensor(
                out=x_shifted[:, c, points], in0=group[:], scalar=bn_scale[:, c : c + 1],
                in1=x_shifted[:, c, points], op0=ALU.mult, op1=ALU.add,
            )
            nc.sync.dma_start(out=out[0][c * P : (c + 1) * P, points], in_=x_shifted[:, c, points])

        all_points = slice(0, POINTS)
        halves = [slice(0, POINTS // 2), slice(POINTS // 2, POINTS)]
        last_acc = []

        def open_last_acc():
            group = bank_pool.tile([P, POINTS // 2], F32, name="last_acc", tag="bank")
            last_acc.append(group)

        regroup_g(0)
        quantise_a(0)
        quantise_g(0)
        for b in range(1, POINT_BLOCKS):
            quantise_a(b)
        regroup_g(1)
        for s in range(-2, ROUNDS):
            if 0 <= s + 1 < ROUNDS:
                quantise_y(s + 1)
            if s + 3 < ROUNDS:
                quantise_g(s + 3)
            if s + 4 < ROUNDS:
                regroup_g(s + 4)
            if s + 1 == ROUNDS - 1:
                prepare_batch_norm()
            lag = max(0, FIRST_STEP_LAG - s)
            if s == ROUNDS - 1:
                open_last_acc()
                for g in range(EARLY_PASSES):
                    second_product(g, STREAM_TILES, halves[0], last_acc[0])
            for i in range(STREAM_TILES + lag):
                if s >= 0 and i < STREAM_TILES:
                    second_product(s, i, all_points, acc[i])
                if 0 <= i - lag < POINT_BLOCKS and s + 2 < ROUNDS:
                    first_product(s + 2, i - lag)
        for c in range(STREAM_TILES):
            finish(c, all_points, acc[c])

        for h in range(2):
            if h > 0:
                open_last_acc()
            for g in range(EARLY_PASSES if h == 0 else 0, ROUNDS):
                second_product(g, STREAM_TILES, halves[h], last_acc[h])
            finish(STREAM_TILES, halves[h], last_acc[h])
